import numpy as np
import ml_dtypes

BF16 = ml_dtypes.bfloat16


def bf(x):
    return np.asarray(x, np.float32).astype(BF16)


def f32(x):
    return np.asarray(x, np.float32)


def f64(x):
    return np.asarray(x).astype(np.float64)


def striped(idx):
    return np.tile(idx.reshape(-1, 16).T, (8, 1))


C, S, N = 128, 2048, 256
MOM = 0.5


def setup_inputs():
    return {"memory": f32(np.random.standard_normal((C, S))), "v": f32(np.random.standard_normal((C, N))), "offs": striped(np.random.permutation(S)[:N])}


def reference(memory, v, offs):
    idx = offs[:16].T.reshape(-1)
    p = MOM * f64(memory)[:, idx] + (1.0 - MOM) * f64(v)
    return p / np.sqrt(np.sum(p * p, axis=0, keepdims=True))

@@ -1,0 +1,42 @@
+import concourse.mybir as mybir
+
+C, S, N = 128, 2048, 256
+F32, BF16, U16 = mybir.dt.float32, mybir.dt.bfloat16, mybir.dt.uint16
+ADD, MULT = mybir.AluOpType.add, mybir.AluOpType.mult
+ACT = mybir.ActivationFunctionType
+
+FLOPS = 6 * C * N
+
+
+def tile_contrastmemory_kernel(tc, memory, v, offs, out):
+    nc = tc.nc
+    with (
+        tc.tile_pool(name="held", bufs=1) as held,
+        tc.psum_pool(name="psum", bufs=1) as psum,
+    ):
+        offsets = held.tile([C, N // 16], U16, name="offsets")
+        nc.sync.dma_start(offsets[:], offs)
+        bank = held.tile([C, S], F32, name="bank")
+        nc.sync.dma_start(bank[:], memory)
+        fresh = held.tile([C, N], F32, name="fresh")
+        nc.scalar.dma_start(fresh[:], v)
+
+        ones = held.tile([C, C], BF16, name="ones")
+        nc.vector.memset(ones[:], 1.0)
+
+        blend = held.tile([C, N], F32, name="blend")
+        nc.vector.tensor_tensor(blend[:], bank[:].indirect(offsets[:]), fresh[:], ADD)
+
+        squares = held.tile([C, N], BF16, name="squares")
+        nc.scalar.activation(squares[:], blend[:], ACT.Square)
+        length2 = psum.tile([C, N], F32, name="length2")
+        nc.tensor.matmul(length2[:], ones[:], squares[:], start=True, stop=True)
+
+        length = held.tile([C, N], F32, name="length")
+        nc.scalar.activation(length[:], length2[:], ACT.Sqrt)
+        inverse = held.tile([C, N], F32, name="inverse")
+        nc.vector.reciprocal(inverse[:], length[:])
+
+        unit = held.tile([C, N], F32, name="unit")
+        nc.vector.tensor_tensor(unit[:], blend[:], inverse[:], MULT)
+        nc.sync.dma_start(out, unit[:])

@@ -28,14 +28,12 @@ def tile_contrastmemory_kernel(tc, memory, v, offs, out):
         nc.vector.tensor_tensor(blend[:], bank[:].indirect(offsets[:]), fresh[:], ADD)
 
         squares = held.tile([C, N], BF16, name="squares")
-        nc.scalar.activation(squares[:], blend[:], ACT.Square)
+        nc.vector.tensor_tensor(squares[:], blend[:], blend[:], MULT)
         length2 = psum.tile([C, N], F32, name="length2")
         nc.tensor.matmul(length2[:], ones[:], squares[:], start=True, stop=True)
 
-        length = held.tile([C, N], F32, name="length")
-        nc.scalar.activation(length[:], length2[:], ACT.Sqrt)
         inverse = held.tile([C, N], F32, name="inverse")
-        nc.vector.reciprocal(inverse[:], length[:])
+        nc.scalar.activation(inverse[:], length2[:], ACT.Abs_reciprocal_sqrt)
 
         unit = held.tile([C, N], F32, name="unit")
         nc.vector.tensor_tensor(unit[:], blend[:], inverse[:], MULT)

@@ -7,6 +7,9 @@ ACT = mybir.ActivationFunctionType
 
 FLOPS = 6 * C * N
 
+PIECE = N // 2
+PIECES = N // PIECE
+
 
 def tile_contrastmemory_kernel(tc, memory, v, offs, out):
     nc = tc.nc
@@ -24,17 +27,27 @@ def tile_contrastmemory_kernel(tc, memory, v, offs, out):
         ones = held.tile([C, C], BF16, name="ones")
         nc.vector.memset(ones[:], 1.0)
 
+        scratch = held.tile([C, 1], F32, name="scratch")
+        nc.vector.memset(scratch[:], 1.0)
+        nc.scalar.activation(scratch[:], scratch[:], ACT.Abs_reciprocal_sqrt)
+
         blend = held.tile([C, N], F32, name="blend")
-        nc.vector.tensor_tensor(blend[:], bank[:].indirect(offsets[:]), fresh[:], ADD)
-
         squares = held.tile([C, N], BF16, name="squares")
-        nc.vector.tensor_tensor(squares[:], blend[:], blend[:], MULT)
-        length2 = psum.tile([C, N], F32, name="length2")
-        nc.tensor.matmul(length2[:], ones[:], squares[:], start=True, stop=True)
-
         inverse = held.tile([C, N], F32, name="inverse")
-        nc.scalar.activation(inverse[:], length2[:], ACT.Abs_reciprocal_sqrt)
-
         unit = held.tile([C, N], F32, name="unit")
-        nc.vector.tensor_tensor(unit[:], blend[:], inverse[:], MULT)
-        nc.sync.dma_start(out, unit[:])
+        length2 = [psum.tile([C, PIECE], F32, name=f"length2_{k}") for k in range(PIECES)]
+        columns = [slice(k * PIECE, (k + 1) * PIECE) for k in range(PIECES)]
+
+        for k in range(PIECES):
+            picked = bank[:].indirect(offsets[:, k * PIECE // 16 : (k + 1) * PIECE // 16])
+            nc.vector.tensor_tensor(blend[:, columns[k]], picked, fresh[:, columns[k]], ADD)
+        for k in range(PIECES):
+            nc.scalar.activation(squares[:, columns[k]], blend[:, columns[k]], ACT.Square)
+        for k in range(PIECES):
+            nc.tensor.matmul(length2[k][:], ones[:], squares[:, columns[k]], start=True, stop=True)
+        for k in range(PIECES):
+            nc.scalar.activation(inverse[:, columns[k]], length2[k][:], ACT.Abs_reciprocal_sqrt)
+        for k in range(PIECES):
+            nc.vector.tensor_tensor(unit[:, columns[k]], blend[:, columns[k]], inverse[:, columns[k]], MULT)
+            queue = nc.sync if k % 2 == 0 else nc.scalar
+            queue.dma_start(out[:, columns[k]], unit[:, columns[k]])

@@ -20,7 +20,8 @@ def tile_contrastmemory_kernel(tc, memory, v, offs, out):
         offsets = held.tile([C, N // 16], U16, name="offsets")
         nc.sync.dma_start(offsets[:], offs)
         bank = held.tile([C, S], F32, name="bank")
-        nc.sync.dma_start(bank[:], memory)
+        nc.sync.dma_start(bank[:, : S // 2], memory[:, : S // 2])
+        nc.scalar.dma_start(bank[:, S // 2 :], memory[:, S // 2 :])
         fresh = held.tile([C, N], F32, name="fresh")
         nc.scalar.dma_start(fresh[:], v)
 

@@ -7,7 +7,7 @@ ACT = mybir.ActivationFunctionType
 
 FLOPS = 6 * C * N
 
-PIECE = N // 2
+PIECE = N // 4
 PIECES = N // PIECE
 
 
@@ -20,8 +20,7 @@ def tile_contrastmemory_kernel(tc, memory, v, offs, out):
         offsets = held.tile([C, N // 16], U16, name="offsets")
         nc.sync.dma_start(offsets[:], offs)
         bank = held.tile([C, S], F32, name="bank")
-        nc.sync.dma_start(bank[:, : S // 2], memory[:, : S // 2])
-        nc.scalar.dma_start(bank[:, S // 2 :], memory[:, S // 2 :])
+        nc.sync.dma_start(bank[:], memory)
         fresh = held.tile([C, N], F32, name="fresh")
         nc.scalar.dma_start(fresh[:], v)
 

@@ -20,7 +20,8 @@ def tile_contrastmemory_kernel(tc, memory, v, offs, out):
         offsets = held.tile([C, N // 16], U16, name="offsets")
         nc.sync.dma_start(offsets[:], offs)
         bank = held.tile([C, S], F32, name="bank")
-        nc.sync.dma_start(bank[:], memory)
+        nc.sync.dma_start(bank[:, : S // 2], memory[:, : S // 2])
+        nc.scalar.dma_start(bank[:, S // 2 :], memory[:, S // 2 :])
         fresh = held.tile([C, N], F32, name="fresh")
         nc.scalar.dma_start(fresh[:], v)
 

@@ -50,5 +50,4 @@ def tile_contrastmemory_kernel(tc, memory, v, offs, out):
             nc.scalar.activation(inverse[:, columns[k]], length2[k][:], ACT.Abs_reciprocal_sqrt)
         for k in range(PIECES):
             nc.vector.tensor_tensor(unit[:, columns[k]], blend[:, columns[k]], inverse[:, columns[k]], MULT)
-            queue = nc.sync if k % 2 == 0 else nc.scalar
-            queue.dma_start(out[:, columns[k]], unit[:, columns[k]])
+            nc.sync.dma_start(out[:, columns[k]], unit[:, columns[k]])

@@ -20,10 +20,9 @@ def tile_contrastmemory_kernel(tc, memory, v, offs, out):
         offsets = held.tile([C, N // 16], U16, name="offsets")
         nc.sync.dma_start(offsets[:], offs)
         bank = held.tile([C, S], F32, name="bank")
-        nc.sync.dma_start(bank[:, : S // 2], memory[:, : S // 2])
-        nc.scalar.dma_start(bank[:, S // 2 :], memory[:, S // 2 :])
+        nc.scalar.dma_start(bank[:], memory)
         fresh = held.tile([C, N], F32, name="fresh")
-        nc.scalar.dma_start(fresh[:], v)
+        nc.sync.dma_start(fresh[:], v)
 
         ones = held.tile([C, C], BF16, name="ones")
         nc.vector.memset(ones[:], 1.0)

@@ -41,8 +41,10 @@ def tile_contrastmemory_kernel(tc, memory, v, offs, out):
         for k in range(PIECES):
             picked = bank[:].indirect(offsets[:, k * PIECE // 16 : (k + 1) * PIECE // 16])
             nc.vector.tensor_tensor(blend[:, columns[k]], picked, fresh[:, columns[k]], ADD)
-        for k in range(PIECES):
+        for k in range(PIECES // 2):
             nc.scalar.activation(squares[:, columns[k]], blend[:, columns[k]], ACT.Square)
+        for k in range(PIECES // 2, PIECES):
+            nc.vector.tensor_tensor(squares[:, columns[k]], blend[:, columns[k]], blend[:, columns[k]], MULT)
         for k in range(PIECES):
             nc.tensor.matmul(length2[k][:], ones[:], squares[:, columns[k]], start=True, stop=True)
         for k in range(PIECES):

@@ -21,8 +21,9 @@ def tile_contrastmemory_kernel(tc, memory, v, offs, out):
         nc.sync.dma_start(offsets[:], offs)
         bank = held.tile([C, S], F32, name="bank")
         nc.scalar.dma_start(bank[:], memory)
-        fresh = held.tile([C, N], F32, name="fresh")
-        nc.sync.dma_start(fresh[:], v)
+        fresh = [held.tile([C, N // 2], F32, name=f"fresh_{h}") for h in range(2)]
+        nc.sync.dma_start(fresh[0][:], v[:, : N // 2])
+        nc.scalar.dma_start(fresh[1][:], v[:, N // 2 :])
 
         ones = held.tile([C, C], BF16, name="ones")
         nc.vector.memset(ones[:], 1.0)
@@ -40,7 +41,8 @@ def tile_contrastmemory_kernel(tc, memory, v, offs, out):
 
         for k in range(PIECES):
             picked = bank[:].indirect(offsets[:, k * PIECE // 16 : (k + 1) * PIECE // 16])
-            nc.vector.tensor_tensor(blend[:, columns[k]], picked, fresh[:, columns[k]], ADD)
+            new = fresh[k // 2][:, (k % 2) * PIECE : (k % 2 + 1) * PIECE]
+            nc.vector.tensor_tensor(blend[:, columns[k]], picked, new, ADD)
         for k in range(PIECES // 2):
             nc.scalar.activation(squares[:, columns[k]], blend[:, columns[k]], ACT.Square)
         for k in range(PIECES // 2, PIECES):

@@ -53,4 +53,6 @@ def tile_contrastmemory_kernel(tc, memory, v, offs, out):
             nc.scalar.activation(inverse[:, columns[k]], length2[k][:], ACT.Abs_reciprocal_sqrt)
         for k in range(PIECES):
             nc.vector.tensor_tensor(unit[:, columns[k]], blend[:, columns[k]], inverse[:, columns[k]], MULT)
-            nc.sync.dma_start(out[:, columns[k]], unit[:, columns[k]])
+            if k % 2 == 1:
+                pair = slice((k - 1) * PIECE, (k + 1) * PIECE)
+                nc.sync.dma_start(out[:, pair], unit[:, pair])

@@ -9,6 +9,7 @@ FLOPS = 6 * C * N
 
 PIECE = N // 4
 PIECES = N // PIECE
+BURST = 256
 
 
 def tile_contrastmemory_kernel(tc, memory, v, offs, out):
@@ -19,9 +20,9 @@ def tile_contrastmemory_kernel(tc, memory, v, offs, out):
     ):
         offsets = held.tile([C, N // 16], U16, name="offsets")
         nc.sync.dma_start(offsets[:], offs)
-        bank = held.tile([C, S], F32, name="bank")
+        bank = held.tile([C, S], F32, name="bank", align_bytes=BURST)
         nc.scalar.dma_start(bank[:], memory)
-        fresh = [held.tile([C, N // 2], F32, name=f"fresh_{h}") for h in range(2)]
+        fresh = [held.tile([C, N // 2], F32, name=f"fresh_{h}", align_bytes=BURST) for h in range(2)]
         nc.sync.dma_start(fresh[0][:], v[:, : N // 2])
         nc.scalar.dma_start(fresh[1][:], v[:, N // 2 :])
 
@@ -35,7 +36,7 @@ def tile_contrastmemory_kernel(tc, memory, v, offs, out):
         blend = held.tile([C, N], F32, name="blend")
         squares = held.tile([C, N], BF16, name="squares")
         inverse = held.tile([C, N], F32, name="inverse")
-        unit = held.tile([C, N], F32, name="unit")
+        unit = held.tile([C, N], F32, name="unit", align_bytes=BURST)
         length2 = [psum.tile([C, PIECE], F32, name=f"length2_{k}") for k in range(PIECES)]
         columns = [slice(k * PIECE, (k + 1) * PIECE) for k in range(PIECES)]
 

@@ -54,6 +54,4 @@ def tile_contrastmemory_kernel(tc, memory, v, offs, out):
             nc.scalar.activation(inverse[:, columns[k]], length2[k][:], ACT.Abs_reciprocal_sqrt)
         for k in range(PIECES):
             nc.vector.tensor_tensor(unit[:, columns[k]], blend[:, columns[k]], inverse[:, columns[k]], MULT)
-            if k % 2 == 1:
-                pair = slice((k - 1) * PIECE, (k + 1) * PIECE)
-                nc.sync.dma_start(out[:, pair], unit[:, pair])
+            nc.sync.dma_start(out[:, columns[k]], unit[:, columns[k]])

import concourse.mybir as mybir

C, S, N = 128, 2048, 256
F32, BF16, U16 = mybir.dt.float32, mybir.dt.bfloat16, mybir.dt.uint16
ADD, MULT = mybir.AluOpType.add, mybir.AluOpType.mult
ACT = mybir.ActivationFunctionType

FLOPS = 6 * C * N

PIECE = N // 4
PIECES = N // PIECE
BURST = 256


def tile_contrastmemory_kernel(tc, memory, v, offs, out):
    nc = tc.nc
    with (
        tc.tile_pool(name="held", bufs=1) as held,
        tc.psum_pool(name="psum", bufs=1) as psum,
    ):
        offsets = held.tile([C, N // 16], U16, name="offsets")
        nc.sync.dma_start(offsets[:], offs)
        bank = held.tile([C, S], F32, name="bank", align_bytes=BURST)
        nc.scalar.dma_start(bank[:], memory)
        fresh = [held.tile([C, N // 2], F32, name=f"fresh_{h}", align_bytes=BURST) for h in range(2)]
        nc.sync.dma_start(fresh[0][:], v[:, : N // 2])
        nc.scalar.dma_start(fresh[1][:], v[:, N // 2 :])

        ones = held.tile([C, C], BF16, name="ones")
        nc.vector.memset(ones[:], 1.0)

        scratch = held.tile([C, 1], F32, name="scratch")
        nc.vector.memset(scratch[:], 1.0)
        nc.scalar.activation(scratch[:], scratch[:], ACT.Abs_reciprocal_sqrt)

        blend = held.tile([C, N], F32, name="blend")
        squares = held.tile([C, N], BF16, name="squares")
        inverse = held.tile([C, N], F32, name="inverse")
        unit = held.tile([C, N], F32, name="unit", align_bytes=BURST)
        length2 = [psum.tile([C, PIECE], F32, name=f"length2_{k}") for k in range(PIECES)]
        columns = [slice(k * PIECE, (k + 1) * PIECE) for k in range(PIECES)]

        for k in range(PIECES):
            picked = bank[:].indirect(offsets[:, k * PIECE // 16 : (k + 1) * PIECE // 16])
            new = fresh[k // 2][:, (k % 2) * PIECE : (k % 2 + 1) * PIECE]
            nc.vector.tensor_tensor(blend[:, columns[k]], picked, new, ADD)
        for k in range(PIECES // 2):
            nc.scalar.activation(squares[:, columns[k]], blend[:, columns[k]], ACT.Square)
        for k in range(PIECES // 2, PIECES):
            nc.vector.tensor_tensor(squares[:, columns[k]], blend[:, columns[k]], blend[:, columns[k]], MULT)
        for k in range(PIECES):
            nc.tensor.matmul(length2[k][:], ones[:], squares[:, columns[k]], start=True, stop=True)
        for k in range(PIECES):
            nc.scalar.activation(inverse[:, columns[k]], length2[k][:], ACT.Abs_reciprocal_sqrt)
        for k in range(PIECES):
            nc.vector.tensor_tensor(unit[:, columns[k]], blend[:, columns[k]], inverse[:, columns[k]], MULT)
            nc.sync.dma_start(out[:, columns[k]], unit[:, columns[k]])
